import numpy as np
import ml_dtypes


def mxq(x, axis, fmt="e4m3"):
    dtype, down = {"e4m3": (ml_dtypes.float8_e4m3fn, 7), "e5m2": (ml_dtypes.float8_e5m2, 14)}[fmt]
    v = np.moveaxis(np.asarray(x, np.float32).astype(ml_dtypes.bfloat16).astype(np.float64), axis, -1)
    blocks = v.reshape(v.shape[:-1] + (-1, 32))
    amax = np.abs(blocks).max(-1, keepdims=True)
    byte = np.maximum(np.where(amax > 0, np.frexp(amax)[1] - 1 + 127, 0) - down, 1)
    scale = np.exp2(byte - 127.0)
    codes = (blocks / scale).astype(np.float32).astype(dtype).astype(np.float64)
    return np.moveaxis((codes * scale).reshape(v.shape), -1, axis)


WIDE = False


def mx_kscale(k):
    if not WIDE:
        return np.ones(k)
    levels = np.array([18, -18])
    if k % 512:
        return np.exp2(np.random.permutation(np.resize(levels, k // 32))).repeat(32)
    a = np.empty((k // 512, 16))
    for p in range(k // 512):
        a[p, :8] = np.random.permutation(np.resize(levels, 8))
        for g in range(8):
            far = levels[np.abs(levels - a[p, g]) >= 10]
            a[p, g + 8] = far[np.random.randint(len(far))]
    return np.exp2(a.ravel()).repeat(32)


BF16 = ml_dtypes.bfloat16


def bf(x):
    return np.asarray(x, np.float32).astype(BF16)


def f64(x):
    return np.asarray(x).astype(np.float64)


B, N, G, KT = 1, 1024, 512, 4


def preactivation(x_taps, h_taps, S, weight_A, weight_B, bias_A, bias_B):
    pre = f64(bias_A) + f64(bias_B)
    for taps, w in ((f64(x_taps), f64(weight_A)), (f64(h_taps), f64(weight_B))):
        last = taps[:, KT - 2] @ f64(S)
        z = np.concatenate([taps, last[:, None]], axis=1).reshape(B, KT * G, N)
        pre = pre + w.reshape(G, KT * G) @ z
    return pre


def setup_inputs():
    s = mx_kscale(2 * G)
    sa, sb = s[:G], s[G:]
    u = mx_kscale(G)
    v = mx_kscale(N)
    c = np.ones(KT)
    c[:KT - 1] = 1.0 / np.max(v)
    x0 = bf(np.random.standard_normal((B, KT - 1, G, N)))
    h0 = bf(np.random.standard_normal((B, KT - 1, G, N)))
    S0 = bf(np.random.standard_normal((B, N, N)) / np.sqrt(N))
    wa0 = bf(np.random.standard_normal((G, KT, G)) / np.sqrt(KT * G))
    wb0 = bf(np.random.standard_normal((G, KT, G)) / np.sqrt(KT * G))
    bias_A = bf(np.random.standard_normal(G) * 0.3)[:, None]
    bias_B = bf(np.random.standard_normal(G) * 0.3)[:, None]
    pre = preactivation(x0, h0, S0, wa0, wb0, bias_A, bias_B)
    g = np.random.standard_normal((B, G, N)) * np.exp2(np.random.randint(-6, 1, (B, 1, N))) * 8.0
    g = g * (np.abs(pre) > 1e-4)
    return {"x_taps": bf(f64(x0) * sa[None, None, :, None]),
            "h_taps": bf(f64(h0) * sb[None, None, :, None]),
            "S": bf(f64(S0) / v[None, None, :]),
            "weight_A": bf(f64(wa0) * c[None, :, None] / sa[None, None, :] / u[:, None, None]),
            "weight_B": bf(f64(wb0) / sb[None, None, :] / u[:, None, None]),
            "bias_A": bias_A,
            "bias_B": bias_B,
            "pre": np.asarray(pre, np.float32),
            "grad_out": bf(g * u[None, :, None] * v[None, None, :])}


def reference(x_taps, h_taps, S, weight_A, weight_B, bias_A, bias_B, pre, grad_out):
    dpre = f64(grad_out) * (f64(pre) > 0.0)
    w = np.concatenate([f64(weight_A).reshape(G, KT * G), f64(weight_B)[:, KT - 1]], axis=1)
    d = mxq(w, 0, "e4m3").T @ mxq(dpre, 1, "e5m2")
    d3 = d[:, (KT - 1) * G:]
    back = mxq(d3[:, :G], 2, "e5m2") @ mxq(f64(S), 2, "e4m3").transpose(0, 2, 1)
    xh = np.concatenate([f64(x_taps)[:, KT - 2], f64(h_taps)[:, KT - 2]], axis=1)
    dS = mxq(xh, 1, "e4m3").transpose(0, 2, 1) @ mxq(d3, 1, "e5m2")
    dx = np.array(d[:, :(KT - 1) * G]).reshape(B, KT - 1, G, N)
    dx[:, KT - 2] = dx[:, KT - 2] + back
    return dx, dS

@@ -1,0 +1,256 @@
+from contextlib import ExitStack
+
+import concourse.mybir as mybir
+from concourse.masks import make_identity
+
+F32 = mybir.dt.float32
+BF16 = mybir.dt.bfloat16
+U32 = mybir.dt.uint32
+U8 = mybir.dt.uint8
+E4M3 = mybir.dt.float8_e4m3fn_x4
+E5M2 = mybir.dt.float8_e5m2_x4
+ALU = mybir.AluOpType
+
+P = 128
+PACK = 4
+G = 512
+N = 1024
+HALF = 512
+TAPS = 4
+X, H = 0, 1
+
+FLOPS = 2 * (G * (TAPS + 1) * G * N + G * N * N + 2 * G * N * N)
+BYTES = 2 * (2 * G * N + N * N + TAPS * G * G + G * G + G * N) + 4 * G * N + 4 * (3 * G * N + N * N)
+
+
+def tile_graphfilterrnnbatch_pb_v_kernel(
+    tc, x_taps, h_taps, S, weight_A, weight_B, bias_A, bias_B, pre, grad_out, out_0, out_1
+):
+    nc = tc.nc
+
+    def copy(engine, out, in_):
+        if engine == "S":
+            nc.scalar.copy(out=out, in_=in_)
+        else:
+            nc.vector.tensor_copy(out=out, in_=in_)
+
+    def interleave(engine, dst, src):
+        copy(engine, dst.rearrange("p (c i) j -> p c j i", i=4), src.rearrange("p j (c i) -> p c j i", i=4))
+
+    with ExitStack() as ctx:
+        keep = ctx.enter_context(tc.tile_pool(name="keep", bufs=1))
+        stage = ctx.enter_context(tc.tile_pool(name="stage", bufs=6))
+        outs = ctx.enter_context(tc.tile_pool(name="outs", bufs=14))
+        psum = ctx.enter_context(tc.psum_pool(name="psum", bufs=8))
+
+        pre_sb = [keep.tile([P, PACK, HALF], F32, name="pre%d" % h, align_bytes=64) for h in range(2)]
+        grad_sb = [keep.tile([P, PACK, HALF], BF16, name="grad%d" % h, align_bytes=64) for h in range(2)]
+        w3_sb = [keep.tile([P, PACK, G], BF16, name="w3_%d" % s, align_bytes=64) for s in range(2)]
+        wa_sb = keep.tile([P, PACK, 3, G], BF16, name="wa", align_bytes=64)
+        xh_sb = [keep.tile([P, PACK, N], BF16, name="xh%d" % s, align_bytes=64) for s in range(2)]
+        s_sb = [keep.tile([P, 2, N], BF16, name="s%d" % q, align_bytes=64) for q in range(4)]
+        pre_v = pre[0, :, :].rearrange("(p j) n -> p j n", j=PACK)
+        grad_v = grad_out[0, :, :].rearrange("(p j) n -> p j n", j=PACK)
+
+        def load_dp(h):
+            cols = slice(h * HALF, (h + 1) * HALF)
+            nc.sync.dma_start(out=pre_sb[h][:], in_=pre_v[:, :, cols])
+            nc.sync.dma_start(out=grad_sb[h][:], in_=grad_v[:, :, cols])
+
+        load_dp(0)
+        nc.sync.dma_start(out=w3_sb[X][:], in_=weight_A[:, 3, :].rearrange("(p j) c -> p j c", j=PACK))
+        nc.sync.dma_start(out=w3_sb[H][:], in_=weight_B[:, 3, :].rearrange("(p j) c -> p j c", j=PACK))
+        nc.sync.dma_start(out=xh_sb[X][:], in_=x_taps[0, 2, :, :].rearrange("(p j) n -> p j n", j=PACK))
+        load_dp(1)
+        nc.sync.dma_start(out=xh_sb[H][:], in_=h_taps[0, 2, :, :].rearrange("(p j) n -> p j n", j=PACK))
+        nc.sync.dma_start(out=wa_sb[:], in_=weight_A[:, 0:3, :].rearrange("(p j) k c -> p j k c", j=PACK))
+        for q in range(4):
+            nc.sync.dma_start(out=s_sb[q][:], in_=S[0, 256 * q : 256 * (q + 1), :].rearrange("(r p) n -> p r n", p=P))
+
+        ident = keep.tile([P, P], F32, name="ident", align_bytes=64)
+        make_identity(nc, ident[:])
+        warm = keep.tile([P, 2], F32, name="warm", align_bytes=64)
+        nc.vector.memset(warm[:, 0:1], 0.0)
+        nc.scalar.copy(out=warm[:, 1:2], in_=warm[:, 0:1])
+
+        def operand(name, cols):
+            codes = keep.tile([P, cols], U32, name=name + "_codes", align_bytes=64)
+            scales = keep.tile([P, cols], U8, name=name + "_scales", align_bytes=64)
+            return codes, scales
+
+        w_q = [operand("w%d" % k, G) for k in range(3)]
+        w3_q = [operand("w3q%d" % s, G) for s in range(2)]
+        dp_q = [operand("dp%d" % h, HALF) for h in range(2)]
+        xh_q = [[operand("xh%d%d" % (s, h), HALF) for h in range(2)] for s in range(2)]
+        d3_q = [[operand("d3%d%d" % (s, h), HALF) for h in range(2)] for s in range(2)]
+        dxt_q = [operand("dxt%d" % g, G) for g in range(2)]
+        st_q = [[operand("st%d%d" % (g, h), HALF) for h in range(2)] for g in range(2)]
+
+        def new_group():
+            grouped = stage.tile([P, HALF, PACK], BF16, name="grouped", align_bytes=64)
+            return grouped
+
+        def quantise(op, grouped, fmt):
+            nc.vector.quantize_mx(
+                out=op[0][:].bitcast(fmt), scales=op[1][:], in_=grouped[:].rearrange("p c j -> p (c j)")
+            )
+
+        def mm(bank, left, lcols, lfmt, right, rfmt, start, stop):
+            nc.tensor.matmul_mx(
+                out=bank[:],
+                lhsT=left[0][:, lcols].bitcast(lfmt),
+                lhsT_scale=left[1][:, lcols],
+                rhs=right[0][:].bitcast(rfmt),
+                rhs_scale=right[1][:],
+                start=start,
+                stop=stop,
+            )
+
+        def block(i):
+            return slice(P * i, P * (i + 1))
+
+        def bank_tile():
+            bank = psum.tile([P, HALF], F32, name="bank")
+            return bank
+
+        def permuted_w(engine, src):
+            g = new_group()
+            copy(engine, g[:].rearrange("p (t m) j -> p t m j", t=4), src.rearrange("p j (m t) -> p t m j", t=4))
+            return g
+
+        def make_dp(h):
+            g = new_group()
+            nc.vector.scalar_tensor_tensor(
+                out=g[:],
+                in0=pre_sb[h][:].rearrange("p j c -> p c j"),
+                scalar=0.0,
+                in1=grad_sb[h][:].rearrange("p j c -> p c j"),
+                op0=ALU.is_gt,
+                op1=ALU.mult,
+            )
+            return g
+
+        d3_sb = [[keep.tile([P, 4, HALF], BF16, name="d3sb%d%d" % (s, h), align_bytes=64) for h in range(2)] for s in range(2)]
+
+        def make_d3(s, h, engines):
+            for t in range(4):
+                bank = bank_tile()
+                mm(bank, w3_q[s], block(t), E4M3, dp_q[h], E5M2, True, True)
+                copy(engines[t], d3_sb[s][h][:, t, :], bank[:])
+
+        def quantise_d3(s, h, engine):
+            g = new_group()
+            interleave(engine, g[:], d3_sb[s][h][:])
+            quantise(d3_q[s][h], g, E5M2)
+
+        def transpose_dx(h, engines):
+            words = d3_sb[X][h][:].rearrange("p t n -> p (t n)").bitcast(F32)
+            g = new_group()
+            gw = g[:].rearrange("p c j -> p (c j)").bitcast(F32).rearrange("p (c u) -> p c u", u=2)
+            for b in range(2):
+                bank = psum.tile([P, 2, 2, P], F32, name="bank")
+                for tt in range(2):
+                    t = 2 * b + tt
+                    for u in range(2):
+                        nc.tensor.transpose(bank[:, tt, u, :], words[:, 256 * t + u : 256 * (t + 1) : 2], ident[:])
+                copy(
+                    engines[b],
+                    gw[:, 256 * b : 256 * (b + 1), :].rearrange("p (t c) u -> p t c u", t=2),
+                    bank[:].rearrange("p t u c -> p t c u"),
+                )
+            quantise(dxt_q[h], g, E5M2)
+
+        def quantise_xh(s, h, engine):
+            g = new_group()
+            interleave(engine, g[:], xh_sb[s][:, :, h * HALF : (h + 1) * HALF])
+            quantise(xh_q[s][h], g, E4M3)
+
+        def transpose_s(g, h, engines):
+            grp = new_group()
+            gw = grp[:].rearrange("p c j -> p (c j)").bitcast(F32).rearrange("p (c u) -> p c u", u=2)
+            for b in range(2):
+                words = s_sb[2 * h + b][:].rearrange("p r n -> p (r n)").bitcast(F32)
+                bank = psum.tile([P, 2, 2, P], F32, name="bank")
+                for r in range(2):
+                    for u in range(2):
+                        lo = 512 * r + 256 * g
+                        nc.tensor.transpose(bank[:, r, u, :], words[:, lo + u : lo + 256 : 2], ident[:])
+                copy(
+                    engines[b],
+                    gw[:, 256 * b : 256 * (b + 1), :].rearrange("p (r c) u -> p r c u", r=2),
+                    bank[:].rearrange("p r u c -> p r c u"),
+                )
+            quantise(st_q[g][h], grp, E4M3)
+
+        def out_tile():
+            o = outs.tile([P, N], F32, name="o", align_bytes=64)
+            return o
+
+        def d_rows(tap, i, engines):
+            o = out_tile()
+            for h in range(2):
+                bank = bank_tile()
+                mm(bank, w_q[tap], block(i), E4M3, dp_q[h], E5M2, True, True)
+                copy(engines[h], o[:, h * HALF : (h + 1) * HALF], bank[:])
+            nc.sync.dma_start(out=out_0[0, tap, P * i : P * (i + 1), :], in_=o[:])
+
+        out_tap2 = out_0[0, 2, :, :].rearrange("(p t) n -> p t n", t=4)
+
+        def tap2_rows(t, engines):
+            o = out_tile()
+            for h in range(2):
+                bank = bank_tile()
+                mm(bank, w_q[2], block(t), E4M3, dp_q[h], E5M2, True, False)
+                for g in range(2):
+                    mm(bank, dxt_q[g], block(t), E5M2, st_q[g][h], E4M3, False, g == 1)
+                copy(engines[h], o[:, h * HALF : (h + 1) * HALF], bank[:])
+            nc.sync.dma_start(out=out_tap2[:, t, :], in_=o[:])
+
+        def ds_rows(i, engines):
+            o = out_tile()
+            for h in range(2):
+                bank = bank_tile()
+                for s in range(2):
+                    mm(bank, xh_q[s][i // 4], block(i % 4), E4M3, d3_q[s][h], E5M2, s == 0, s == 1)
+                copy(engines[h], o[:, h * HALF : (h + 1) * HALF], bank[:])
+            nc.sync.dma_start(out=out_1[0, P * i : P * (i + 1), :], in_=o[:])
+
+        dp0 = make_dp(0)
+        g3 = permuted_w("V", w3_sb[X][:])
+        gb = permuted_w("S", w3_sb[H][:])
+        quantise(dp_q[0], dp0, E5M2)
+        quantise(w3_q[X], g3, E4M3)
+        make_d3(X, 0, "SSSS")
+        quantise(w3_q[H], gb, E4M3)
+        make_d3(H, 0, "SSSS")
+        quantise_xh(X, 0, "V")
+        quantise_d3(X, 0, "V")
+        dp1 = make_dp(1)
+        quantise(dp_q[1], dp1, E5M2)
+        make_d3(X, 1, "SSSS")
+        make_d3(H, 1, "SSSS")
+        quantise_d3(H, 0, "V")
+        quantise_d3(X, 1, "V")
+        quantise_d3(H, 1, "V")
+        quantise_xh(H, 0, "V")
+        transpose_dx(0, "SS")
+        transpose_dx(1, "SS")
+        for i in range(4):
+            ds_rows(i, "SS")
+        for tap in range(2):
+            g = new_group()
+            interleave("V", g[:], wa_sb[:, :, tap, :])
+            quantise(w_q[tap], g, E4M3)
+            for i in range(4):
+                d_rows(tap, i, "SS")
+        quantise_xh(X, 1, "V")
+        quantise_xh(H, 1, "V")
+        for i in range(4, 8):
+            ds_rows(i, "SS")
+        g = permuted_w("V", wa_sb[:, :, 2, :])
+        quantise(w_q[2], g, E4M3)
+        for h in range(2):
+            for g in range(2):
+                transpose_s(g, h, "VV")
+        for t in range(4):
+            tap2_rows(t, "SV")

@@ -9,18 +9,25 @@ U32 = mybir.dt.uint32
 U8 = mybir.dt.uint8
 E4M3 = mybir.dt.float8_e4m3fn_x4
 E5M2 = mybir.dt.float8_e5m2_x4
-ALU = mybir.AluOpType
+IS_GT = mybir.AluOpType.is_gt
+MULT = mybir.AluOpType.mult
 
 P = 128
 PACK = 4
-G = 512
-N = 1024
+FEATURES = 512
+NODES = 1024
 HALF = 512
+QUARTER = 256
 TAPS = 4
+LAST_TAP = 3
 X, H = 0, 1
 
-FLOPS = 2 * (G * (TAPS + 1) * G * N + G * N * N + 2 * G * N * N)
-BYTES = 2 * (2 * G * N + N * N + TAPS * G * G + G * G + G * N) + 4 * G * N + 4 * (3 * G * N + N * N)
+FLOPS = 2 * ((TAPS + 1) * FEATURES * FEATURES * NODES + FEATURES * NODES * NODES + 2 * FEATURES * NODES * NODES)
+BYTES = (
+    2 * (2 * FEATURES * NODES + NODES * NODES + (TAPS + 1) * FEATURES * FEATURES + FEATURES * NODES)
+    + 4 * FEATURES * NODES
+    + 4 * (3 * FEATURES * NODES + NODES * NODES)
+)
 
 
 def tile_graphfilterrnnbatch_pb_v_kernel(
@@ -28,229 +35,320 @@ def tile_graphfilterrnnbatch_pb_v_kernel(
 ):
     nc = tc.nc
 
-    def copy(engine, out, in_):
-        if engine == "S":
-            nc.scalar.copy(out=out, in_=in_)
-        else:
-            nc.vector.tensor_copy(out=out, in_=in_)
+    def on_vector(out, in_):
+        nc.vector.tensor_copy(out=out, in_=in_)
 
-    def interleave(engine, dst, src):
-        copy(engine, dst.rearrange("p (c i) j -> p c j i", i=4), src.rearrange("p j (c i) -> p c j i", i=4))
+    def on_scalar(out, in_):
+        nc.scalar.copy(out=out, in_=in_)
+
+    V, A = on_vector, on_scalar
 
     with ExitStack() as ctx:
         keep = ctx.enter_context(tc.tile_pool(name="keep", bufs=1))
-        stage = ctx.enter_context(tc.tile_pool(name="stage", bufs=6))
-        outs = ctx.enter_context(tc.tile_pool(name="outs", bufs=14))
+        groups = ctx.enter_context(tc.tile_pool(name="groups", bufs=8))
+        rows = ctx.enter_context(tc.tile_pool(name="rows", bufs=14))
         psum = ctx.enter_context(tc.psum_pool(name="psum", bufs=8))
 
-        pre_sb = [keep.tile([P, PACK, HALF], F32, name="pre%d" % h, align_bytes=64) for h in range(2)]
-        grad_sb = [keep.tile([P, PACK, HALF], BF16, name="grad%d" % h, align_bytes=64) for h in range(2)]
-        w3_sb = [keep.tile([P, PACK, G], BF16, name="w3_%d" % s, align_bytes=64) for s in range(2)]
-        wa_sb = keep.tile([P, PACK, 3, G], BF16, name="wa", align_bytes=64)
-        xh_sb = [keep.tile([P, PACK, N], BF16, name="xh%d" % s, align_bytes=64) for s in range(2)]
-        s_sb = [keep.tile([P, 2, N], BF16, name="s%d" % q, align_bytes=64) for q in range(4)]
-        pre_v = pre[0, :, :].rearrange("(p j) n -> p j n", j=PACK)
-        grad_v = grad_out[0, :, :].rearrange("(p j) n -> p j n", j=PACK)
+        def half(h):
+            return slice(h * HALF, (h + 1) * HALF)
 
-        def load_dp(h):
-            cols = slice(h * HALF, (h + 1) * HALF)
-            nc.sync.dma_start(out=pre_sb[h][:], in_=pre_v[:, :, cols])
-            nc.sync.dma_start(out=grad_sb[h][:], in_=grad_v[:, :, cols])
+        def block(i):
+            return slice(i * P, (i + 1) * P)
 
-        load_dp(0)
-        nc.sync.dma_start(out=w3_sb[X][:], in_=weight_A[:, 3, :].rearrange("(p j) c -> p j c", j=PACK))
-        nc.sync.dma_start(out=w3_sb[H][:], in_=weight_B[:, 3, :].rearrange("(p j) c -> p j c", j=PACK))
-        nc.sync.dma_start(out=xh_sb[X][:], in_=x_taps[0, 2, :, :].rearrange("(p j) n -> p j n", j=PACK))
-        load_dp(1)
-        nc.sync.dma_start(out=xh_sb[H][:], in_=h_taps[0, 2, :, :].rearrange("(p j) n -> p j n", j=PACK))
-        nc.sync.dma_start(out=wa_sb[:], in_=weight_A[:, 0:3, :].rearrange("(p j) k c -> p j k c", j=PACK))
-        for q in range(4):
-            nc.sync.dma_start(out=s_sb[q][:], in_=S[0, 256 * q : 256 * (q + 1), :].rearrange("(r p) n -> p r n", p=P))
+        def by_four(ap):
+            return ap.rearrange("(p j) n -> p j n", j=PACK)
 
-        ident = keep.tile([P, P], F32, name="ident", align_bytes=64)
-        make_identity(nc, ident[:])
-        warm = keep.tile([P, 2], F32, name="warm", align_bytes=64)
-        nc.vector.memset(warm[:, 0:1], 0.0)
-        nc.scalar.copy(out=warm[:, 1:2], in_=warm[:, 0:1])
+        pre_sb = [keep.tile([P, PACK, HALF], F32, name="pre_%d" % h, align_bytes=64) for h in range(2)]
+        grad_sb = [keep.tile([P, PACK, HALF], BF16, name="grad_%d" % h, align_bytes=64) for h in range(2)]
+        w_sb = [keep.tile([P, PACK, FEATURES], BF16, name="w_%d" % k, align_bytes=64) for k in range(TAPS + 1)]
+        xh_sb = [keep.tile([P, PACK, NODES], BF16, name="xh_%d" % s, align_bytes=64) for s in (X, H)]
+        s_sb = [keep.tile([P, 2, NODES], BF16, name="s_%d" % c, align_bytes=64) for c in range(4)]
 
-        def operand(name, cols):
-            codes = keep.tile([P, cols], U32, name=name + "_codes", align_bytes=64)
-            scales = keep.tile([P, cols], U8, name=name + "_scales", align_bytes=64)
-            return codes, scales
+        def load_pre(h, lo, hi):
+            nc.sync.dma_start(out=pre_sb[h][:, :, lo:hi], in_=by_four(pre[0, :, h * HALF + lo : h * HALF + hi]))
 
-        w_q = [operand("w%d" % k, G) for k in range(3)]
-        w3_q = [operand("w3q%d" % s, G) for s in range(2)]
-        dp_q = [operand("dp%d" % h, HALF) for h in range(2)]
-        xh_q = [[operand("xh%d%d" % (s, h), HALF) for h in range(2)] for s in range(2)]
-        d3_q = [[operand("d3%d%d" % (s, h), HALF) for h in range(2)] for s in range(2)]
-        dxt_q = [operand("dxt%d" % g, G) for g in range(2)]
-        st_q = [[operand("st%d%d" % (g, h), HALF) for h in range(2)] for g in range(2)]
+        def load_grad(h, lo, hi):
+            nc.sync.dma_start(out=grad_sb[h][:, :, lo:hi], in_=by_four(grad_out[0, :, h * HALF + lo : h * HALF + hi]))
 
-        def new_group():
-            grouped = stage.tile([P, HALF, PACK], BF16, name="grouped", align_bytes=64)
-            return grouped
+        def load_w(k):
+            source = weight_A[:, k, :] if k < TAPS else weight_B[:, LAST_TAP, :]
+            nc.sync.dma_start(out=w_sb[k][:], in_=by_four(source))
 
-        def quantise(op, grouped, fmt):
-            nc.vector.quantize_mx(
-                out=op[0][:].bitcast(fmt), scales=op[1][:], in_=grouped[:].rearrange("p c j -> p (c j)")
+        def load_xh(s):
+            source = x_taps if s == X else h_taps
+            nc.sync.dma_start(out=xh_sb[s][:], in_=by_four(source[0, 2, :, :]))
+
+        def load_s(c):
+            nc.sync.dma_start(
+                out=s_sb[c][:], in_=S[0, 2 * P * c : 2 * P * (c + 1), :].rearrange("(r p) n -> p r n", p=P)
             )
 
-        def mm(bank, left, lcols, lfmt, right, rfmt, start, stop):
+        load_w(1)
+        load_w(3)
+        load_grad(0, 0, QUARTER)
+        load_pre(0, 0, QUARTER)
+        load_pre(0, QUARTER, HALF)
+        load_grad(0, QUARTER, HALF)
+        load_w(0)
+        load_w(4)
+        load_pre(1, 0, HALF)
+        load_grad(1, 0, HALF)
+        load_s(2)
+        load_s(3)
+        load_xh(X)
+        load_w(2)
+        load_xh(H)
+        load_s(0)
+        load_s(1)
+
+        identity = keep.tile([P, P], F32, name="identity", align_bytes=64)
+        make_identity(nc, identity[:])
+        first = keep.tile([P, 2], F32, name="first", align_bytes=64)
+        nc.vector.memset(first[:, 0:1], 0.0)
+        nc.scalar.copy(out=first[:, 1:2], in_=first[:, 0:1])
+
+        def operand(name):
+            codes = keep.tile([P, HALF], U32, name=name + "_codes", align_bytes=64)
+            scales = keep.tile([P, HALF], U8, name=name + "_scales", align_bytes=64)
+            return codes, scales
+
+        w_q = [operand("wq_%d" % k) for k in range(TAPS + 1)]
+        dpre_q = [operand("dpre_%d" % h) for h in range(2)]
+        xh_q = [[operand("xhq_%d%d" % (s, h)) for h in range(2)] for s in (X, H)]
+        d3_q = [[operand("d3q_%d%d" % (s, h)) for h in range(2)] for s in (X, H)]
+        dx3t_q = [operand("dx3t_%d" % g) for g in range(2)]
+        st_q = [[operand("st_%d%d" % (g, h)) for h in range(2)] for g in range(2)]
+
+        def new_group():
+            group = groups.tile([P, HALF, PACK], BF16, name="group", align_bytes=64)
+            return group
+
+        def quantise(target, group, dtype):
+            nc.vector.quantize_mx(
+                out=target[0][:].bitcast(dtype), scales=target[1][:], in_=group[:].rearrange("p c j -> p (c j)")
+            )
+
+        def matmul(bank, left, columns, left_dtype, right, right_dtype, start, stop):
             nc.tensor.matmul_mx(
                 out=bank[:],
-                lhsT=left[0][:, lcols].bitcast(lfmt),
-                lhsT_scale=left[1][:, lcols],
-                rhs=right[0][:].bitcast(rfmt),
+                lhsT=left[0][:, columns].bitcast(left_dtype),
+                lhsT_scale=left[1][:, columns],
+                rhs=right[0][:].bitcast(right_dtype),
                 rhs_scale=right[1][:],
                 start=start,
                 stop=stop,
             )
 
-        def block(i):
-            return slice(P * i, P * (i + 1))
-
-        def bank_tile():
+        def new_bank():
             bank = psum.tile([P, HALF], F32, name="bank")
             return bank
 
-        def permuted_w(engine, src):
-            g = new_group()
-            copy(engine, g[:].rearrange("p (t m) j -> p t m j", t=4), src.rearrange("p j (m t) -> p t m j", t=4))
-            return g
+        def interleave(engine, group, source):
+            engine(group.rearrange("p (c i) j -> p c j i", i=4), source.rearrange("p j (c i) -> p c j i", i=4))
 
-        def make_dp(h):
-            g = new_group()
+        def mask(group, h, lo, hi):
             nc.vector.scalar_tensor_tensor(
-                out=g[:],
-                in0=pre_sb[h][:].rearrange("p j c -> p c j"),
+                out=group[:, lo:hi, :],
+                in0=pre_sb[h][:, :, lo:hi].rearrange("p j c -> p c j"),
                 scalar=0.0,
-                in1=grad_sb[h][:].rearrange("p j c -> p c j"),
-                op0=ALU.is_gt,
-                op1=ALU.mult,
+                in1=grad_sb[h][:, :, lo:hi].rearrange("p j c -> p c j"),
+                op0=IS_GT,
+                op1=MULT,
             )
-            return g
 
-        d3_sb = [[keep.tile([P, 4, HALF], BF16, name="d3sb%d%d" % (s, h), align_bytes=64) for h in range(2)] for s in range(2)]
+        def mix_w(k, engine):
+            group = new_group()
+            if k < 2:
+                interleave(engine, group[:], w_sb[k][:])
+            else:
+                engine(
+                    group[:].rearrange("p (t m) j -> p t m j", t=4), w_sb[k][:].rearrange("p j (m t) -> p t m j", t=4)
+                )
+            return lambda: quantise(w_q[k], group, E4M3)
+
+        def mix_xh(s, h, engine):
+            group = new_group()
+            interleave(engine, group[:], xh_sb[s][:, :, half(h)])
+            return lambda: quantise(xh_q[s][h], group, E4M3)
+
+        d3_sb = [
+            [keep.tile([P, PACK, HALF], BF16, name="d3_%d%d" % (s, h), align_bytes=64) for h in range(2)] for s in (X, H)
+        ]
 
         def make_d3(s, h, engines):
-            for t in range(4):
-                bank = bank_tile()
-                mm(bank, w3_q[s], block(t), E4M3, dp_q[h], E5M2, True, True)
-                copy(engines[t], d3_sb[s][h][:, t, :], bank[:])
+            for t in range(PACK):
+                bank = new_bank()
+                matmul(bank, w_q[LAST_TAP + s], block(t), E4M3, dpre_q[h], E5M2, True, True)
+                engines[t](
+                    d3_sb[s][h][:, t, :].rearrange("p (u q e) -> p u q e", u=2, e=2),
+                    bank[:].rearrange("p (q u e) -> p u q e", u=2, e=2),
+                )
 
-        def quantise_d3(s, h, engine):
-            g = new_group()
-            interleave(engine, g[:], d3_sb[s][h][:])
-            quantise(d3_q[s][h], g, E5M2)
+        def mix_d3(s, h, engine):
+            group = new_group()
+            interleave(engine, group[:], d3_sb[s][h][:])
+            return lambda: quantise(d3_q[s][h], group, E5M2)
 
-        def transpose_dx(h, engines):
-            words = d3_sb[X][h][:].rearrange("p t n -> p (t n)").bitcast(F32)
-            g = new_group()
-            gw = g[:].rearrange("p c j -> p (c j)").bitcast(F32).rearrange("p (c u) -> p c u", u=2)
+        def words_of(tile):
+            return tile[:].rearrange("p a b -> p (a b)").bitcast(F32)
+
+        def transpose_dx3(h, engines):
+            words = words_of(d3_sb[X][h])
+            group = new_group()
+            pairs = words_of(group).rearrange("p (c u) -> p c u", u=2)
             for b in range(2):
                 bank = psum.tile([P, 2, 2, P], F32, name="bank")
-                for tt in range(2):
-                    t = 2 * b + tt
+                for i in range(2):
                     for u in range(2):
-                        nc.tensor.transpose(bank[:, tt, u, :], words[:, 256 * t + u : 256 * (t + 1) : 2], ident[:])
-                copy(
-                    engines[b],
-                    gw[:, 256 * b : 256 * (b + 1), :].rearrange("p (t c) u -> p t c u", t=2),
-                    bank[:].rearrange("p t u c -> p t c u"),
+                        nc.tensor.transpose(bank[:, i, u, :], words[:, block(4 * b + 2 * i + u)], identity[:])
+                engines[b](
+                    pairs[:, 2 * P * b : 2 * P * (b + 1), :].rearrange("p (i c) u -> p i c u", i=2),
+                    bank[:].rearrange("p i u c -> p i c u"),
                 )
-            quantise(dxt_q[h], g, E5M2)
-
-        def quantise_xh(s, h, engine):
-            g = new_group()
-            interleave(engine, g[:], xh_sb[s][:, :, h * HALF : (h + 1) * HALF])
-            quantise(xh_q[s][h], g, E4M3)
+            return lambda: quantise(dx3t_q[h], group, E5M2)
 
         def transpose_s(g, h, engines):
-            grp = new_group()
-            gw = grp[:].rearrange("p c j -> p (c j)").bitcast(F32).rearrange("p (c u) -> p c u", u=2)
+            group = new_group()
+            pairs = words_of(group).rearrange("p (c u) -> p c u", u=2)
             for b in range(2):
-                words = s_sb[2 * h + b][:].rearrange("p r n -> p (r n)").bitcast(F32)
+                words = words_of(s_sb[2 * h + b])
                 bank = psum.tile([P, 2, 2, P], F32, name="bank")
                 for r in range(2):
                     for u in range(2):
-                        lo = 512 * r + 256 * g
-                        nc.tensor.transpose(bank[:, r, u, :], words[:, lo + u : lo + 256 : 2], ident[:])
-                copy(
-                    engines[b],
-                    gw[:, 256 * b : 256 * (b + 1), :].rearrange("p (r c) u -> p r c u", r=2),
+                        low = (r * NODES + g * HALF) // 2
+                        nc.tensor.transpose(bank[:, r, u, :], words[:, low + u : low + 2 * P : 2], identity[:])
+                engines[b](
+                    pairs[:, 2 * P * b : 2 * P * (b + 1), :].rearrange("p (r c) u -> p r c u", r=2),
                     bank[:].rearrange("p r u c -> p r c u"),
                 )
-            quantise(st_q[g][h], grp, E4M3)
+            return lambda: quantise(st_q[g][h], group, E4M3)
 
-        def out_tile():
-            o = outs.tile([P, N], F32, name="o", align_bytes=64)
-            return o
+        open_rows = {}
 
-        def d_rows(tap, i, engines):
-            o = out_tile()
-            for h in range(2):
-                bank = bank_tile()
-                mm(bank, w_q[tap], block(i), E4M3, dp_q[h], E5M2, True, True)
-                copy(engines[h], o[:, h * HALF : (h + 1) * HALF], bank[:])
-            nc.sync.dma_start(out=out_0[0, tap, P * i : P * (i + 1), :], in_=o[:])
+        def emit(key, h, engine, bank, target, pair_order=False, by_halves=False):
+            first_half = key not in open_rows
+            if first_half:
+                open_rows[key] = rows.tile([P, NODES], F32, name="row", align_bytes=64)
+            row = open_rows[key]
+            if pair_order:
+                engine(
+                    row[:, half(h)].rearrange("p (q u e) -> p q u e", u=2, e=2),
+                    bank[:].rearrange("p (u q e) -> p q u e", u=2, e=2),
+                )
+            else:
+                engine(row[:, half(h)], bank[:])
+            if by_halves:
+                nc.sync.dma_start(out=target[:, half(h)], in_=row[:, half(h)])
+            elif not first_half:
+                nc.sync.dma_start(out=target, in_=row[:])
 
-        out_tap2 = out_0[0, 2, :, :].rearrange("(p t) n -> p t n", t=4)
+        def direct(tap, i, h, engine):
+            bank = new_bank()
+            matmul(bank, w_q[tap], block(i), E4M3, dpre_q[h], E5M2, True, True)
+            emit((tap, i), h, engine, bank, out_0[0, tap, block(i), :])
 
-        def tap2_rows(t, engines):
-            o = out_tile()
-            for h in range(2):
-                bank = bank_tile()
-                mm(bank, w_q[2], block(t), E4M3, dp_q[h], E5M2, True, False)
-                for g in range(2):
-                    mm(bank, dxt_q[g], block(t), E5M2, st_q[g][h], E4M3, False, g == 1)
-                copy(engines[h], o[:, h * HALF : (h + 1) * HALF], bank[:])
-            nc.sync.dma_start(out=out_tap2[:, t, :], in_=o[:])
+        tap2_rows = out_0[0, 2, :, :].rearrange("(p t) n -> p t n", t=PACK)
 
-        def ds_rows(i, engines):
-            o = out_tile()
-            for h in range(2):
-                bank = bank_tile()
-                for s in range(2):
-                    mm(bank, xh_q[s][i // 4], block(i % 4), E4M3, d3_q[s][h], E5M2, s == 0, s == 1)
-                copy(engines[h], o[:, h * HALF : (h + 1) * HALF], bank[:])
-            nc.sync.dma_start(out=out_1[0, P * i : P * (i + 1), :], in_=o[:])
+        def tap2(t, h, engine):
+            bank = new_bank()
+            matmul(bank, w_q[2], block(t), E4M3, dpre_q[h], E5M2, True, False)
+            matmul(bank, dx3t_q[0], block(t), E5M2, st_q[0][h], E4M3, False, False)
+            matmul(bank, dx3t_q[1], block(t), E5M2, st_q[1][h], E4M3, False, True)
+            emit((2, t), h, engine, bank, tap2_rows[:, t, :], by_halves=t == PACK - 1)
 
-        dp0 = make_dp(0)
-        g3 = permuted_w("V", w3_sb[X][:])
-        gb = permuted_w("S", w3_sb[H][:])
-        quantise(dp_q[0], dp0, E5M2)
-        quantise(w3_q[X], g3, E4M3)
-        make_d3(X, 0, "SSSS")
-        quantise(w3_q[H], gb, E4M3)
-        make_d3(H, 0, "SSSS")
-        quantise_xh(X, 0, "V")
-        quantise_d3(X, 0, "V")
-        dp1 = make_dp(1)
-        quantise(dp_q[1], dp1, E5M2)
-        make_d3(X, 1, "SSSS")
-        make_d3(H, 1, "SSSS")
-        quantise_d3(H, 0, "V")
-        quantise_d3(X, 1, "V")
-        quantise_d3(H, 1, "V")
-        quantise_xh(H, 0, "V")
-        transpose_dx(0, "SS")
-        transpose_dx(1, "SS")
-        for i in range(4):
-            ds_rows(i, "SS")
-        for tap in range(2):
-            g = new_group()
-            interleave("V", g[:], wa_sb[:, :, tap, :])
-            quantise(w_q[tap], g, E4M3)
-            for i in range(4):
-                d_rows(tap, i, "SS")
-        quantise_xh(X, 1, "V")
-        quantise_xh(H, 1, "V")
-        for i in range(4, 8):
-            ds_rows(i, "SS")
-        g = permuted_w("V", wa_sb[:, :, 2, :])
-        quantise(w_q[2], g, E4M3)
-        for h in range(2):
-            for g in range(2):
-                transpose_s(g, h, "VV")
-        for t in range(4):
-            tap2_rows(t, "SV")
+        def shift(i, h, engine):
+            bank = new_bank()
+            for s in (X, H):
+                matmul(bank, xh_q[s][i // 4], block(i % 4), E4M3, d3_q[s][h], E5M2, s == X, s == H)
+            emit(("shift", i), h, engine, bank, out_1[0, block(i), :], pair_order=True)
+
+        with tc.manual_schedule():
+            quantise_w3 = mix_w(3, A)
+            quantise_w1 = mix_w(1, V)
+            quantise_w1()
+            dpre_0 = new_group()
+            mask(dpre_0, 0, 0, QUARTER)
+            quantise_w3()
+            quantise_w0 = mix_w(0, A)
+            mask(dpre_0, 0, QUARTER, HALF)
+            quantise(dpre_q[0], dpre_0, E5M2)
+            quantise_w4 = mix_w(4, V)
+            make_d3(X, 0, (A, V, A, A))
+            direct(1, 0, 0, A)
+            quantise_w4()
+            quantise_w0()
+            direct(1, 1, 0, A)
+            direct(1, 2, 0, V)
+            make_d3(H, 0, (A, A, A, A))
+            quantise_dx0 = transpose_dx3(0, (A, A))
+            dpre_1 = new_group()
+            mask(dpre_1, 1, 0, HALF)
+            quantise_st01 = transpose_s(0, 1, (V, A))
+            quantise(dpre_q[1], dpre_1, E5M2)
+            direct(1, 3, 0, A)
+            direct(1, 0, 1, A)
+            quantise_d3h0 = mix_d3(H, 0, V)
+            direct(1, 1, 1, A)
+            quantise_d3x0 = mix_d3(X, 0, V)
+            quantise_d3h0()
+            quantise_x0 = mix_xh(X, 0, V)
+            direct(1, 2, 1, A)
+            make_d3(X, 1, (A, A, A, A))
+            quantise_d3x0()
+            quantise_h0 = mix_xh(H, 0, V)
+            quantise_d3x1 = mix_d3(X, 1, V)
+            quantise_st11 = transpose_s(1, 1, (A, A))
+            quantise_x0()
+            make_d3(H, 1, (A, V, A, A))
+            quantise_h0()
+            quantise_d3h1 = mix_d3(H, 1, V)
+            direct(1, 3, 1, A)
+            quantise_d3x1()
+            quantise_dx1 = transpose_dx3(1, (A, A))
+            direct(0, 0, 0, A)
+            quantise_d3h1()
+            quantise_h1 = mix_xh(H, 1, V)
+            quantise_st00 = transpose_s(0, 0, (A, V))
+            quantise_x1 = mix_xh(X, 1, V)
+            direct(0, 1, 0, A)
+            direct(0, 0, 1, A)
+            quantise_h1()
+            direct(0, 1, 1, A)
+            quantise_x1()
+            quantise_st10 = transpose_s(1, 0, (A, V))
+            quantise_w2 = mix_w(2, V)
+            shift(0, 0, A)
+            shift(0, 1, A)
+            shift(1, 0, A)
+            shift(1, 1, A)
+            shift(2, 0, A)
+            shift(2, 1, A)
+            shift(3, 0, A)
+            quantise_dx0()
+            quantise_st10()
+            shift(3, 1, A)
+            direct(0, 2, 0, A)
+            direct(0, 2, 1, A)
+            shift(4, 0, A)
+            quantise_dx1()
+            shift(4, 1, A)
+            shift(5, 0, A)
+            quantise_w2()
+            quantise_st00()
+            quantise_st11()
+            quantise_st01()
+            shift(5, 1, A)
+            shift(6, 0, A)
+            shift(6, 1, A)
+            shift(7, 0, V)
+            shift(7, 1, A)
+            direct(0, 3, 0, V)
+            direct(0, 3, 1, A)
+            tap2(0, 0, A)
+            tap2(0, 1, V)
+            tap2(1, 0, A)
+            tap2(1, 1, V)
+            tap2(2, 0, V)
+            tap2(2, 1, V)
+            tap2(3, 0, V)
+            tap2(3, 1, V)

from contextlib import ExitStack

import concourse.mybir as mybir
from concourse.masks import make_identity

F32 = mybir.dt.float32
BF16 = mybir.dt.bfloat16
U32 = mybir.dt.uint32
U8 = mybir.dt.uint8
E4M3 = mybir.dt.float8_e4m3fn_x4
E5M2 = mybir.dt.float8_e5m2_x4
IS_GT = mybir.AluOpType.is_gt
MULT = mybir.AluOpType.mult

P = 128
PACK = 4
FEATURES = 512
NODES = 1024
HALF = 512
QUARTER = 256
TAPS = 4
LAST_TAP = 3
X, H = 0, 1

FLOPS = 2 * ((TAPS + 1) * FEATURES * FEATURES * NODES + FEATURES * NODES * NODES + 2 * FEATURES * NODES * NODES)
BYTES = (
    2 * (2 * FEATURES * NODES + NODES * NODES + (TAPS + 1) * FEATURES * FEATURES + FEATURES * NODES)
    + 4 * FEATURES * NODES
    + 4 * (3 * FEATURES * NODES + NODES * NODES)
)


def tile_graphfilterrnnbatch_pb_v_kernel(
    tc, x_taps, h_taps, S, weight_A, weight_B, bias_A, bias_B, pre, grad_out, out_0, out_1
):
    nc = tc.nc

    def on_vector(out, in_):
        nc.vector.tensor_copy(out=out, in_=in_)

    def on_scalar(out, in_):
        nc.scalar.copy(out=out, in_=in_)

    V, A = on_vector, on_scalar

    with ExitStack() as ctx:
        keep = ctx.enter_context(tc.tile_pool(name="keep", bufs=1))
        groups = ctx.enter_context(tc.tile_pool(name="groups", bufs=8))
        rows = ctx.enter_context(tc.tile_pool(name="rows", bufs=14))
        psum = ctx.enter_context(tc.psum_pool(name="psum", bufs=8))

        def half(h):
            return slice(h * HALF, (h + 1) * HALF)

        def block(i):
            return slice(i * P, (i + 1) * P)

        def by_four(ap):
            return ap.rearrange("(p j) n -> p j n", j=PACK)

        pre_sb = [keep.tile([P, PACK, HALF], F32, name="pre_%d" % h, align_bytes=64) for h in range(2)]
        grad_sb = [keep.tile([P, PACK, HALF], BF16, name="grad_%d" % h, align_bytes=64) for h in range(2)]
        w_sb = [keep.tile([P, PACK, FEATURES], BF16, name="w_%d" % k, align_bytes=64) for k in range(TAPS + 1)]
        xh_sb = [keep.tile([P, PACK, NODES], BF16, name="xh_%d" % s, align_bytes=64) for s in (X, H)]
        s_sb = [keep.tile([P, 2, NODES], BF16, name="s_%d" % c, align_bytes=64) for c in range(4)]

        def load_pre(h, lo, hi):
            nc.sync.dma_start(out=pre_sb[h][:, :, lo:hi], in_=by_four(pre[0, :, h * HALF + lo : h * HALF + hi]))

        def load_grad(h, lo, hi):
            nc.sync.dma_start(out=grad_sb[h][:, :, lo:hi], in_=by_four(grad_out[0, :, h * HALF + lo : h * HALF + hi]))

        def load_w(k):
            source = weight_A[:, k, :] if k < TAPS else weight_B[:, LAST_TAP, :]
            nc.sync.dma_start(out=w_sb[k][:], in_=by_four(source))

        def load_xh(s):
            source = x_taps if s == X else h_taps
            nc.sync.dma_start(out=xh_sb[s][:], in_=by_four(source[0, 2, :, :]))

        def load_s(c):
            nc.sync.dma_start(
                out=s_sb[c][:], in_=S[0, 2 * P * c : 2 * P * (c + 1), :].rearrange("(r p) n -> p r n", p=P)
            )

        load_w(1)
        load_w(3)
        load_grad(0, 0, QUARTER)
        load_pre(0, 0, QUARTER)
        load_pre(0, QUARTER, HALF)
        load_grad(0, QUARTER, HALF)
        load_w(0)
        load_w(4)
        load_pre(1, 0, HALF)
        load_grad(1, 0, HALF)
        load_s(2)
        load_s(3)
        load_xh(X)
        load_w(2)
        load_xh(H)
        load_s(0)
        load_s(1)

        identity = keep.tile([P, P], F32, name="identity", align_bytes=64)
        make_identity(nc, identity[:])
        first = keep.tile([P, 2], F32, name="first", align_bytes=64)
        nc.vector.memset(first[:, 0:1], 0.0)
        nc.scalar.copy(out=first[:, 1:2], in_=first[:, 0:1])

        def operand(name):
            codes = keep.tile([P, HALF], U32, name=name + "_codes", align_bytes=64)
            scales = keep.tile([P, HALF], U8, name=name + "_scales", align_bytes=64)
            return codes, scales

        w_q = [operand("wq_%d" % k) for k in range(TAPS + 1)]
        dpre_q = [operand("dpre_%d" % h) for h in range(2)]
        xh_q = [[operand("xhq_%d%d" % (s, h)) for h in range(2)] for s in (X, H)]
        d3_q = [[operand("d3q_%d%d" % (s, h)) for h in range(2)] for s in (X, H)]
        dx3t_q = [operand("dx3t_%d" % g) for g in range(2)]
        st_q = [[operand("st_%d%d" % (g, h)) for h in range(2)] for g in range(2)]

        def new_group():
            group = groups.tile([P, HALF, PACK], BF16, name="group", align_bytes=64)
            return group

        def quantise(target, group, dtype):
            nc.vector.quantize_mx(
                out=target[0][:].bitcast(dtype), scales=target[1][:], in_=group[:].rearrange("p c j -> p (c j)")
            )

        def matmul(bank, left, columns, left_dtype, right, right_dtype, start, stop):
            nc.tensor.matmul_mx(
                out=bank[:],
                lhsT=left[0][:, columns].bitcast(left_dtype),
                lhsT_scale=left[1][:, columns],
                rhs=right[0][:].bitcast(right_dtype),
                rhs_scale=right[1][:],
                start=start,
                stop=stop,
            )

        def new_bank():
            bank = psum.tile([P, HALF], F32, name="bank")
            return bank

        def interleave(engine, group, source):
            engine(group.rearrange("p (c i) j -> p c j i", i=4), source.rearrange("p j (c i) -> p c j i", i=4))

        def mask(group, h, lo, hi):
            nc.vector.scalar_tensor_tensor(
                out=group[:, lo:hi, :],
                in0=pre_sb[h][:, :, lo:hi].rearrange("p j c -> p c j"),
                scalar=0.0,
                in1=grad_sb[h][:, :, lo:hi].rearrange("p j c -> p c j"),
                op0=IS_GT,
                op1=MULT,
            )

        def mix_w(k, engine):
            group = new_group()
            if k < 2:
                interleave(engine, group[:], w_sb[k][:])
            else:
                engine(
                    group[:].rearrange("p (t m) j -> p t m j", t=4), w_sb[k][:].rearrange("p j (m t) -> p t m j", t=4)
                )
            return lambda: quantise(w_q[k], group, E4M3)

        def mix_xh(s, h, engine):
            group = new_group()
            interleave(engine, group[:], xh_sb[s][:, :, half(h)])
            return lambda: quantise(xh_q[s][h], group, E4M3)

        d3_sb = [
            [keep.tile([P, PACK, HALF], BF16, name="d3_%d%d" % (s, h), align_bytes=64) for h in range(2)] for s in (X, H)
        ]

        def make_d3(s, h, engines):
            for t in range(PACK):
                bank = new_bank()
                matmul(bank, w_q[LAST_TAP + s], block(t), E4M3, dpre_q[h], E5M2, True, True)
                engines[t](
                    d3_sb[s][h][:, t, :].rearrange("p (u q e) -> p u q e", u=2, e=2),
                    bank[:].rearrange("p (q u e) -> p u q e", u=2, e=2),
                )

        def mix_d3(s, h, engine):
            group = new_group()
            interleave(engine, group[:], d3_sb[s][h][:])
            return lambda: quantise(d3_q[s][h], group, E5M2)

        def words_of(tile):
            return tile[:].rearrange("p a b -> p (a b)").bitcast(F32)

        def transpose_dx3(h, engines):
            words = words_of(d3_sb[X][h])
            group = new_group()
            pairs = words_of(group).rearrange("p (c u) -> p c u", u=2)
            for b in range(2):
                bank = psum.tile([P, 2, 2, P], F32, name="bank")
                for i in range(2):
                    for u in range(2):
                        nc.tensor.transpose(bank[:, i, u, :], words[:, block(4 * b + 2 * i + u)], identity[:])
                engines[b](
                    pairs[:, 2 * P * b : 2 * P * (b + 1), :].rearrange("p (i c) u -> p i c u", i=2),
                    bank[:].rearrange("p i u c -> p i c u"),
                )
            return lambda: quantise(dx3t_q[h], group, E5M2)

        def transpose_s(g, h, engines):
            group = new_group()
            pairs = words_of(group).rearrange("p (c u) -> p c u", u=2)
            for b in range(2):
                words = words_of(s_sb[2 * h + b])
                bank = psum.tile([P, 2, 2, P], F32, name="bank")
                for r in range(2):
                    for u in range(2):
                        low = (r * NODES + g * HALF) // 2
                        nc.tensor.transpose(bank[:, r, u, :], words[:, low + u : low + 2 * P : 2], identity[:])
                engines[b](
                    pairs[:, 2 * P * b : 2 * P * (b + 1), :].rearrange("p (r c) u -> p r c u", r=2),
                    bank[:].rearrange("p r u c -> p r c u"),
                )
            return lambda: quantise(st_q[g][h], group, E4M3)

        open_rows = {}

        def emit(key, h, engine, bank, target, pair_order=False, by_halves=False):
            first_half = key not in open_rows
            if first_half:
                open_rows[key] = rows.tile([P, NODES], F32, name="row", align_bytes=64)
            row = open_rows[key]
            if pair_order:
                engine(
                    row[:, half(h)].rearrange("p (q u e) -> p q u e", u=2, e=2),
                    bank[:].rearrange("p (u q e) -> p q u e", u=2, e=2),
                )
            else:
                engine(row[:, half(h)], bank[:])
            if by_halves:
                nc.sync.dma_start(out=target[:, half(h)], in_=row[:, half(h)])
            elif not first_half:
                nc.sync.dma_start(out=target, in_=row[:])

        def direct(tap, i, h, engine):
            bank = new_bank()
            matmul(bank, w_q[tap], block(i), E4M3, dpre_q[h], E5M2, True, True)
            emit((tap, i), h, engine, bank, out_0[0, tap, block(i), :])

        tap2_rows = out_0[0, 2, :, :].rearrange("(p t) n -> p t n", t=PACK)

        def tap2(t, h, engine):
            bank = new_bank()
            matmul(bank, w_q[2], block(t), E4M3, dpre_q[h], E5M2, True, False)
            matmul(bank, dx3t_q[0], block(t), E5M2, st_q[0][h], E4M3, False, False)
            matmul(bank, dx3t_q[1], block(t), E5M2, st_q[1][h], E4M3, False, True)
            emit((2, t), h, engine, bank, tap2_rows[:, t, :], by_halves=t == PACK - 1)

        def shift(i, h, engine):
            bank = new_bank()
            for s in (X, H):
                matmul(bank, xh_q[s][i // 4], block(i % 4), E4M3, d3_q[s][h], E5M2, s == X, s == H)
            emit(("shift", i), h, engine, bank, out_1[0, block(i), :], pair_order=True)

        with tc.manual_schedule():
            quantise_w3 = mix_w(3, A)
            quantise_w1 = mix_w(1, V)
            quantise_w1()
            dpre_0 = new_group()
            mask(dpre_0, 0, 0, QUARTER)
            quantise_w3()
            quantise_w0 = mix_w(0, A)
            mask(dpre_0, 0, QUARTER, HALF)
            quantise(dpre_q[0], dpre_0, E5M2)
            quantise_w4 = mix_w(4, V)
            make_d3(X, 0, (A, V, A, A))
            direct(1, 0, 0, A)
            quantise_w4()
            quantise_w0()
            direct(1, 1, 0, A)
            direct(1, 2, 0, V)
            make_d3(H, 0, (A, A, A, A))
            quantise_dx0 = transpose_dx3(0, (A, A))
            dpre_1 = new_group()
            mask(dpre_1, 1, 0, HALF)
            quantise_st01 = transpose_s(0, 1, (V, A))
            quantise(dpre_q[1], dpre_1, E5M2)
            direct(1, 3, 0, A)
            direct(1, 0, 1, A)
            quantise_d3h0 = mix_d3(H, 0, V)
            direct(1, 1, 1, A)
            quantise_d3x0 = mix_d3(X, 0, V)
            quantise_d3h0()
            quantise_x0 = mix_xh(X, 0, V)
            direct(1, 2, 1, A)
            make_d3(X, 1, (A, A, A, A))
            quantise_d3x0()
            quantise_h0 = mix_xh(H, 0, V)
            quantise_d3x1 = mix_d3(X, 1, V)
            quantise_st11 = transpose_s(1, 1, (A, A))
            quantise_x0()
            make_d3(H, 1, (A, V, A, A))
            quantise_h0()
            quantise_d3h1 = mix_d3(H, 1, V)
            direct(1, 3, 1, A)
            quantise_d3x1()
            quantise_dx1 = transpose_dx3(1, (A, A))
            direct(0, 0, 0, A)
            quantise_d3h1()
            quantise_h1 = mix_xh(H, 1, V)
            quantise_st00 = transpose_s(0, 0, (A, V))
            quantise_x1 = mix_xh(X, 1, V)
            direct(0, 1, 0, A)
            direct(0, 0, 1, A)
            quantise_h1()
            direct(0, 1, 1, A)
            quantise_x1()
            quantise_st10 = transpose_s(1, 0, (A, V))
            quantise_w2 = mix_w(2, V)
            shift(0, 0, A)
            shift(0, 1, A)
            shift(1, 0, A)
            shift(1, 1, A)
            shift(2, 0, A)
            shift(2, 1, A)
            shift(3, 0, A)
            quantise_dx0()
            quantise_st10()
            shift(3, 1, A)
            direct(0, 2, 0, A)
            direct(0, 2, 1, A)
            shift(4, 0, A)
            quantise_dx1()
            shift(4, 1, A)
            shift(5, 0, A)
            quantise_w2()
            quantise_st00()
            quantise_st11()
            quantise_st01()
            shift(5, 1, A)
            shift(6, 0, A)
            shift(6, 1, A)
            shift(7, 0, V)
            shift(7, 1, A)
            direct(0, 3, 0, V)
            direct(0, 3, 1, A)
            tap2(0, 0, A)
            tap2(0, 1, V)
            tap2(1, 0, A)
            tap2(1, 1, V)
            tap2(2, 0, V)
            tap2(2, 1, V)
            tap2(3, 0, V)
            tap2(3, 1, V)
